import numpy as np
import ml_dtypes


def mxq(x, axis, fmt="e4m3"):
    dtype, down = {"e4m3": (ml_dtypes.float8_e4m3fn, 7), "e5m2": (ml_dtypes.float8_e5m2, 14)}[fmt]
    v = np.moveaxis(np.asarray(x, np.float32).astype(ml_dtypes.bfloat16).astype(np.float64), axis, -1)
    blocks = v.reshape(v.shape[:-1] + (-1, 32))
    amax = np.abs(blocks).max(-1, keepdims=True)
    byte = np.maximum(np.where(amax > 0, np.frexp(amax)[1] - 1 + 127, 0) - down, 1)
    scale = np.exp2(byte - 127.0)
    codes = (blocks / scale).astype(np.float32).astype(dtype).astype(np.float64)
    return np.moveaxis((codes * scale).reshape(v.shape), -1, axis)


WIDE = False


def mx_kscale(k):
    if not WIDE:
        return np.ones(k)
    levels = np.array([10, -10, 5, -5, 0])
    a = np.random.permutation(np.resize(levels, k // 512 * 4)).reshape(k // 512, 4)
    idx = np.arange(k)
    return np.exp2(a[idx // 512, idx % 128 // 32])


BF16 = ml_dtypes.bfloat16


def bf(x):
    return np.asarray(x, np.float32).astype(BF16)


def f64(x):
    return np.asarray(x).astype(np.float64)


N, D, C, R = 8192, 1024, 128, 128
SCALE = 20.0


def softplus(v):
    return np.logaddexp(v, 0.0)


def inv_softplus(y):
    return y + np.log(-np.expm1(-y))


def setup_inputs():
    s = mx_kscale(D)
    x = np.random.standard_normal((N, D)) * (0.6 + 0.8 * np.random.random_sample((N, 1)))
    var = (2.0 / D) * np.exp(np.random.standard_normal((C, D)) + 0.5 * np.random.standard_normal((C, 1)))
    return {"x": bf(x * s),
            "cls_w": bf(np.random.standard_normal((C, D)) * 0.15 / np.sqrt(D) / s),
            "cls_b": bf(np.random.standard_normal(C) * 0.3),
            "sigma_w": bf(inv_softplus(var / (s * s))),
            "bbox_w": bf(np.random.standard_normal((R, D)) / np.sqrt(D) / s),
            "bbox_b": bf(np.random.standard_normal(R) * 0.3)}


def reference(x, cls_w, cls_b, sigma_w, bbox_w, bbox_b):
    x = f64(x)
    var = softplus(f64(sigma_w))
    xq = mxq(x, 1, "e4m3")
    m = xq @ mxq(f64(cls_w), 1, "e4m3").T
    v = mxq(x * x, 1, "e4m3") @ mxq(var, 1, "e4m3").T
    k = 1.0 / np.sqrt(1.0 + (np.pi / 8.0) * v)
    scores = SCALE * k * m + f64(cls_b)[None, :]
    proposal_deltas = (xq @ mxq(f64(bbox_w), 1, "e4m3").T) + f64(bbox_b)[None, :]
    return scores, proposal_deltas

@@ -1,0 +1,206 @@
+import math
+from contextlib import ExitStack
+
+import concourse.mybir as mybir
+from concourse.masks import make_identity
+
+FLOPS = 3 * 2 * 8192 * 1024 * 128
+
+F32 = mybir.dt.float32
+BF16 = mybir.dt.bfloat16
+U32 = mybir.dt.uint32
+U8 = mybir.dt.uint8
+FP8X4 = mybir.dt.float8_e4m3fn_x4
+ACT = mybir.ActivationFunctionType
+ALU = mybir.AluOpType
+
+P = 128
+D = 1024
+WORDS = D // 2
+J = 4
+QROWS = P * J
+NQ = 8192 // QROWS
+C = 128
+VSPLIT = 1920
+
+
+def tile_bayesianoutputlayers_t_kernel(tc, x, cls_w, cls_b, sigma_w, bbox_w, bbox_b, out_0, out_1):
+    nc = tc.nc
+    with ExitStack() as ctx:
+        const = ctx.enter_context(tc.tile_pool(name="const", bufs=1))
+        prep = ctx.enter_context(tc.tile_pool(name="prep", bufs=1))
+        xin = ctx.enter_context(tc.tile_pool(name="xin", bufs=6))
+        grp = ctx.enter_context(tc.tile_pool(name="grp", bufs=3))
+        cod = ctx.enter_context(tc.tile_pool(name="cod", bufs=3))
+        epi = ctx.enter_context(tc.tile_pool(name="epi", bufs=2))
+        res = ctx.enter_context(tc.tile_pool(name="res", bufs=3))
+        tps = ctx.enter_context(tc.psum_pool(name="tps", bufs=4))
+        mdp = ctx.enter_context(tc.psum_pool(name="mdp", bufs=2))
+        vps = ctx.enter_context(tc.psum_pool(name="vps", bufs=2))
+
+        sg = prep.tile([P, D], BF16, name="sg")
+        nc.sync.dma_start(out=sg[:], in_=sigma_w[:, :])
+        xts = []
+        xt0 = xin.tile([P, J * D], BF16, name="xt")
+        x0v = x[0:QROWS, :].rearrange("(p j) k -> p j k", j=J)
+        for j in range(J):
+            nc.sync.dma_start(out=xt0[:, j * D:(j + 1) * D], in_=x0v[:, j, :])
+            if j == 0:
+                cw = prep.tile([P, D], BF16, name="cw")
+                nc.sync.dma_start(out=cw[:], in_=cls_w[:, :])
+                bw = prep.tile([P, D], BF16, name="bw")
+                nc.sync.dma_start(out=bw[:], in_=bbox_w[:, :])
+        xts.append(xt0)
+        cb16 = prep.tile([P, C], BF16, name="cb16")
+        nc.scalar.dma_start(out=cb16[:], in_=cls_b.partition_broadcast(P))
+        bb16 = prep.tile([P, C], BF16, name="bb16")
+        nc.scalar.dma_start(out=bb16[:], in_=bbox_b.partition_broadcast(P))
+
+        ident = const.tile([P, P], F32, name="ident")
+        make_identity(nc, ident[:])
+
+        def transpose_row_tile(words, bank):
+            for c in range(4):
+                nc.tensor.transpose(bank[:, c * P:(c + 1) * P], words[:, c * P:(c + 1) * P], ident[:])
+
+        def bank_view(bank):
+            return bank[:].rearrange("p (g u r) -> p g r u", g=2, u=2, r=P)
+
+        ab = prep.tile([P, D], F32, name="ab")
+        nc.scalar.activation(out=ab[:], in_=sg[:], func=ACT.Abs)
+        u = prep.tile([P, D], F32, name="u")
+        nc.scalar.activation(out=u[:], in_=ab[:], func=ACT.Exp, scale=-1.0)
+        q4 = prep.tile([P, D], F32, name="q4")
+        nc.scalar.activation(out=q4[:], in_=ab[:], func=ACT.Exp, scale=-4.0, bias=1.0e-6 - math.log(4.0))
+        lb = prep.tile([P, D], F32, name="lb")
+        nc.scalar.activation(out=lb[:], in_=u[:], func=ACT.Ln, scale=1.0, bias=1.0)
+        a1 = prep.tile([P, D], F32, name="a1")
+        nc.vector.tensor_scalar(out=a1[:], in0=u[:], scalar1=1.0 / 3.0, scalar2=-0.5, op0=ALU.mult, op1=ALU.add)
+        a2 = prep.tile([P, D], F32, name="a2")
+        nc.vector.tensor_tensor(out=a2[:], in0=a1[:], in1=u[:], op=ALU.mult)
+        t3 = prep.tile([P, D], F32, name="t3")
+        nc.vector.scalar_tensor_tensor(out=t3[:], in0=a2[:], scalar=1.0, in1=u[:], op0=ALU.add, op1=ALU.mult)
+        t4 = prep.tile([P, D], F32, name="t4")
+        nc.vector.tensor_tensor(out=t4[:], in0=t3[:], in1=q4[:], op=ALU.subtract)
+        m1 = prep.tile([P, D], F32, name="m1")
+        nc.vector.tensor_tensor(out=m1[:], in0=t3[:], in1=lb[:], op=ALU.min)
+        m2 = prep.tile([P, D], F32, name="m2")
+        nc.vector.tensor_tensor(out=m2[:], in0=m1[:], in1=t4[:], op=ALU.max)
+        vr = prep.tile([P, D], BF16, name="vr")
+        nc.vector.scalar_tensor_tensor(out=vr[:], in0=sg[:], scalar=0.0, in1=m2[:], op0=ALU.max, op1=ALU.add)
+
+        wg = const.tile([P, 2 * 2 * C * 4], BF16, name="wg", align_bytes=64)
+        wgw = wg[:].bitcast(F32).rearrange("p (g w c u) -> p g w c u", g=2, w=2, c=C, u=2)
+        for w, src in enumerate((cw, bw)):
+            bank = tps.tile([P, WORDS], F32, name="bank")
+            transpose_row_tile(src[:].bitcast(F32), bank)
+            nc.vector.tensor_copy(out=wgw[:, :, w, :, :], in_=bank_view(bank))
+        wc = const.tile([P, 2 * 2 * C], U32, name="wc", align_bytes=64)
+        ws = const.tile([P, 2 * 2 * C], U8, name="ws", align_bytes=64)
+        nc.vector.quantize_mx(out=wc[:].bitcast(FP8X4), scales=ws[:], in_=wg[:])
+
+        vg = const.tile([P, 2 * C * 4], BF16, name="vg", align_bytes=64)
+        bank = tps.tile([P, WORDS], F32, name="bank")
+        transpose_row_tile(vr[:].bitcast(F32), bank)
+        nc.vector.tensor_copy(
+            out=vg[:].bitcast(F32).rearrange("p (g c u) -> p g c u", g=2, c=C, u=2), in_=bank_view(bank)
+        )
+        vc = const.tile([P, 2 * C], U32, name="vc", align_bytes=64)
+        vs = const.tile([P, 2 * C], U8, name="vs", align_bytes=64)
+        nc.vector.quantize_mx(out=vc[:].bitcast(FP8X4), scales=vs[:], in_=vg[:])
+
+        cbt = const.tile([P, C], F32, name="cbt")
+        nc.vector.tensor_copy(out=cbt[:], in_=cb16[:])
+        bbt = const.tile([P, C], F32, name="bbt")
+        nc.vector.tensor_copy(out=bbt[:], in_=bb16[:])
+
+        for q in range(NQ):
+            rows = slice(q * QROWS, (q + 1) * QROWS)
+            if q == 0:
+                xt = xts[0]
+            else:
+                xt = xin.tile([P, J * D], BF16, name="xt")
+                nc.sync.dma_start(out=xt[:], in_=x[rows, :].rearrange("(p j) k -> p (j k)", j=J))
+            xw = xt[:].bitcast(F32)
+
+            xg = grp.tile([P, J * D], BF16, name="xg", align_bytes=64)
+            xgw = xg[:].bitcast(F32).rearrange("p (j g r u) -> p j g r u", j=J, g=2, r=P, u=2)
+            banks = []
+            for j in range(J):
+                bank = tps.tile([P, WORDS], F32, name="bank")
+                transpose_row_tile(xw[:, j * WORDS:(j + 1) * WORDS], bank)
+                banks.append(bank)
+            for j in range(J):
+                nc.scalar.copy(out=xgw[:, j], in_=bank_view(banks[j]))
+
+            sq = grp.tile([P, J * D], BF16, name="sq", align_bytes=64)
+            nc.vector.tensor_tensor(out=sq[:, :VSPLIT], in0=xg[:, :VSPLIT], in1=xg[:, :VSPLIT], op=ALU.mult)
+            nc.scalar.activation(out=sq[:, VSPLIT:], in_=xg[:, VSPLIT:], func=ACT.Square)
+
+            xc = cod.tile([P, J * 2 * P], U32, name="xc", align_bytes=64)
+            xs = cod.tile([P, J * 2 * P], U8, name="xs", align_bytes=64)
+            nc.vector.quantize_mx(out=xc[:].bitcast(FP8X4), scales=xs[:], in_=xg[:])
+            sc_ = cod.tile([P, J * 2 * P], U32, name="sc_", align_bytes=64)
+            ss = cod.tile([P, J * 2 * P], U8, name="ss", align_bytes=64)
+            nc.vector.quantize_mx(out=sc_[:].bitcast(FP8X4), scales=ss[:], in_=sq[:])
+
+            md = [mdp.tile([P, 512], F32, name="md") for h in range(2)]
+            for j in range(J):
+                for g in range(2):
+                    sl = slice((j * 2 + g) * P, (j * 2 + g + 1) * P)
+                    nc.tensor.matmul_mx(
+                        out=md[j // 2][:, (j % 2) * 256:(j % 2 + 1) * 256],
+                        lhsT=xc[:, sl].bitcast(FP8X4),
+                        lhsT_scale=xs[:, sl],
+                        rhs=wc[:, g * 256:(g + 1) * 256].bitcast(FP8X4),
+                        rhs_scale=ws[:, g * 256:(g + 1) * 256],
+                        start=(g == 0),
+                        stop=(g == 1),
+                    )
+            vb = vps.tile([P, 512], F32, name="vb")
+            for j in range(J):
+                for g in range(2):
+                    sl = slice((j * 2 + g) * P, (j * 2 + g + 1) * P)
+                    nc.tensor.matmul_mx(
+                        out=vb[:, j * C:(j + 1) * C],
+                        lhsT=sc_[:, sl].bitcast(FP8X4),
+                        lhsT_scale=ss[:, sl],
+                        rhs=vc[:, g * C:(g + 1) * C].bitcast(FP8X4),
+                        rhs_scale=vs[:, g * C:(g + 1) * C],
+                        start=(g == 0),
+                        stop=(g == 1),
+                    )
+
+            kk = epi.tile([P, J * C], F32, name="kk")
+            nc.scalar.activation(
+                out=kk[:], in_=vb[:], func=ACT.Abs_reciprocal_sqrt, scale=math.pi / 3200.0, bias=1.0 / 400.0
+            )
+            tm = epi.tile([P, J * C], F32, name="tm")
+            dl = res.tile([P, J * C], F32, name="dl")
+            so = res.tile([P, J * C], F32, name="so")
+            for h in range(2):
+                mdv = md[h][:].rearrange("p (t s c) -> p t s c", t=2, s=2, c=C)
+                hs = slice(h * 2 * C, (h + 1) * 2 * C)
+                nc.vector.tensor_tensor(
+                    out=dl[:, hs].rearrange("p (t c) -> p t c", t=2),
+                    in0=mdv[:, :, 1, :],
+                    in1=bbt[:].unsqueeze(1).to_broadcast([P, 2, C]),
+                    op=ALU.add,
+                )
+            nc.sync.dma_start(out=out_1[rows, :].rearrange("(p j) c -> p (j c)", j=J), in_=dl[:])
+            for h in range(2):
+                mdv = md[h][:].rearrange("p (t s c) -> p t s c", t=2, s=2, c=C)
+                hs = slice(h * 2 * C, (h + 1) * 2 * C)
+                nc.vector.tensor_tensor(
+                    out=tm[:, hs].rearrange("p (t c) -> p t c", t=2),
+                    in0=mdv[:, :, 0, :],
+                    in1=kk[:, hs].rearrange("p (t c) -> p t c", t=2),
+                    op=ALU.mult,
+                )
+            nc.vector.tensor_tensor(
+                out=so[:].rearrange("p (t c) -> p t c", t=J),
+                in0=tm[:].rearrange("p (t c) -> p t c", t=J),
+                in1=cbt[:].unsqueeze(1).to_broadcast([P, J, C]),
+                op=ALU.add,
+            )
+            nc.sync.dma_start(out=out_0[rows, :].rearrange("(p j) c -> p (j c)", j=J), in_=so[:])

@@ -19,9 +19,11 @@ D = 1024
 WORDS = D // 2
 J = 4
 QROWS = P * J
-NQ = 8192 // QROWS
+NQ = 16
 C = 128
-VSPLIT = 1920
+VSPLIT = 2304
+QSA = 896
+PRE = 5
 
 
 def tile_bayesianoutputlayers_t_kernel(tc, x, cls_w, cls_b, sigma_w, bbox_w, bbox_b, out_0, out_1):
@@ -30,27 +32,46 @@ def tile_bayesianoutputlayers_t_kernel(tc, x, cls_w, cls_b, sigma_w, bbox_w, bbo
         const = ctx.enter_context(tc.tile_pool(name="const", bufs=1))
         prep = ctx.enter_context(tc.tile_pool(name="prep", bufs=1))
         xin = ctx.enter_context(tc.tile_pool(name="xin", bufs=6))
-        grp = ctx.enter_context(tc.tile_pool(name="grp", bufs=3))
-        cod = ctx.enter_context(tc.tile_pool(name="cod", bufs=3))
+        grp = ctx.enter_context(tc.tile_pool(name="grp", bufs=2))
+        cod = ctx.enter_context(tc.tile_pool(name="cod", bufs=2))
         epi = ctx.enter_context(tc.tile_pool(name="epi", bufs=2))
         res = ctx.enter_context(tc.tile_pool(name="res", bufs=3))
         tps = ctx.enter_context(tc.psum_pool(name="tps", bufs=4))
-        mdp = ctx.enter_context(tc.psum_pool(name="mdp", bufs=2))
-        vps = ctx.enter_context(tc.psum_pool(name="vps", bufs=2))
+        ops = ctx.enter_context(tc.psum_pool(name="ops", bufs=1))
+        ctx.enter_context(tc.manual_schedule())
+
+        xt = {}
+        xg = {}
+        sq = {}
+        xc = {}
+        xs = {}
+        qc = {}
+        qs = {}
+        banks = {}
+        mb = {}
+        db = {}
+        vb = {}
+        kk = {}
+        tm = {}
+
+        def load(q):
+            xt[q] = xin.tile([P, J * D], BF16, name="xt")
+            rows = x[q * QROWS:(q + 1) * QROWS, :]
+            if q == 0:
+                view = rows.rearrange("(p j) k -> p j k", j=J)
+                for j in range(J):
+                    nc.sync.dma_start(out=xt[q][:, j * D:(j + 1) * D], in_=view[:, j, :])
+            else:
+                nc.sync.dma_start(out=xt[q][:], in_=rows.rearrange("(p j) k -> p (j k)", j=J))
 
         sg = prep.tile([P, D], BF16, name="sg")
         nc.sync.dma_start(out=sg[:], in_=sigma_w[:, :])
-        xts = []
-        xt0 = xin.tile([P, J * D], BF16, name="xt")
-        x0v = x[0:QROWS, :].rearrange("(p j) k -> p j k", j=J)
-        for j in range(J):
-            nc.sync.dma_start(out=xt0[:, j * D:(j + 1) * D], in_=x0v[:, j, :])
-            if j == 0:
-                cw = prep.tile([P, D], BF16, name="cw")
-                nc.sync.dma_start(out=cw[:], in_=cls_w[:, :])
-                bw = prep.tile([P, D], BF16, name="bw")
-                nc.sync.dma_start(out=bw[:], in_=bbox_w[:, :])
-        xts.append(xt0)
+        cw = prep.tile([P, D], BF16, name="cw")
+        nc.sync.dma_start(out=cw[:], in_=cls_w[:, :])
+        bw = prep.tile([P, D], BF16, name="bw")
+        nc.sync.dma_start(out=bw[:], in_=bbox_w[:, :])
+        for q in range(PRE - 2):
+            load(q)
         cb16 = prep.tile([P, C], BF16, name="cb16")
         nc.scalar.dma_start(out=cb16[:], in_=cls_b.partition_broadcast(P))
         bb16 = prep.tile([P, C], BF16, name="bb16")
@@ -58,6 +79,10 @@ def tile_bayesianoutputlayers_t_kernel(tc, x, cls_w, cls_b, sigma_w, bbox_w, bbo
 
         ident = const.tile([P, P], F32, name="ident")
         make_identity(nc, ident[:])
+        cbt = const.tile([P, C], F32, name="cbt")
+        nc.gpsimd.tensor_copy(out=cbt[:], in_=cb16[:])
+        bbt = const.tile([P, C], F32, name="bbt")
+        nc.gpsimd.tensor_copy(out=bbt[:], in_=bb16[:])
 
         def transpose_row_tile(words, bank):
             for c in range(4):
@@ -70,137 +95,175 @@ def tile_bayesianoutputlayers_t_kernel(tc, x, cls_w, cls_b, sigma_w, bbox_w, bbo
         nc.scalar.activation(out=ab[:], in_=sg[:], func=ACT.Abs)
         u = prep.tile([P, D], F32, name="u")
         nc.scalar.activation(out=u[:], in_=ab[:], func=ACT.Exp, scale=-1.0)
+
+        wg = const.tile([P, 2 * 2 * C * 4], BF16, name="wg", align_bytes=64)
+        wgw = wg[:].bitcast(F32).rearrange("p (w g c u) -> p w g c u", w=2, g=2, c=C, u=2)
+        for w, src in enumerate((cw, bw)):
+            wbank = ops.tile([P, WORDS], F32, name="wbank")
+            transpose_row_tile(src[:].bitcast(F32), wbank)
+            nc.scalar.copy(out=wgw[:, w], in_=bank_view(wbank))
         q4 = prep.tile([P, D], F32, name="q4")
         nc.scalar.activation(out=q4[:], in_=ab[:], func=ACT.Exp, scale=-4.0, bias=1.0e-6 - math.log(4.0))
-        lb = prep.tile([P, D], F32, name="lb")
-        nc.scalar.activation(out=lb[:], in_=u[:], func=ACT.Ln, scale=1.0, bias=1.0)
+
         a1 = prep.tile([P, D], F32, name="a1")
         nc.vector.tensor_scalar(out=a1[:], in0=u[:], scalar1=1.0 / 3.0, scalar2=-0.5, op0=ALU.mult, op1=ALU.add)
         a2 = prep.tile([P, D], F32, name="a2")
         nc.vector.tensor_tensor(out=a2[:], in0=a1[:], in1=u[:], op=ALU.mult)
         t3 = prep.tile([P, D], F32, name="t3")
         nc.vector.scalar_tensor_tensor(out=t3[:], in0=a2[:], scalar=1.0, in1=u[:], op0=ALU.add, op1=ALU.mult)
-        t4 = prep.tile([P, D], F32, name="t4")
-        nc.vector.tensor_tensor(out=t4[:], in0=t3[:], in1=q4[:], op=ALU.subtract)
-        m1 = prep.tile([P, D], F32, name="m1")
-        nc.vector.tensor_tensor(out=m1[:], in0=t3[:], in1=lb[:], op=ALU.min)
-        m2 = prep.tile([P, D], F32, name="m2")
-        nc.vector.tensor_tensor(out=m2[:], in0=m1[:], in1=t4[:], op=ALU.max)
-        vr = prep.tile([P, D], BF16, name="vr")
-        nc.vector.scalar_tensor_tensor(out=vr[:], in0=sg[:], scalar=0.0, in1=m2[:], op0=ALU.max, op1=ALU.add)
-
-        wg = const.tile([P, 2 * 2 * C * 4], BF16, name="wg", align_bytes=64)
-        wgw = wg[:].bitcast(F32).rearrange("p (g w c u) -> p g w c u", g=2, w=2, c=C, u=2)
-        for w, src in enumerate((cw, bw)):
-            bank = tps.tile([P, WORDS], F32, name="bank")
-            transpose_row_tile(src[:].bitcast(F32), bank)
-            nc.vector.tensor_copy(out=wgw[:, :, w, :, :], in_=bank_view(bank))
         wc = const.tile([P, 2 * 2 * C], U32, name="wc", align_bytes=64)
         ws = const.tile([P, 2 * 2 * C], U8, name="ws", align_bytes=64)
         nc.vector.quantize_mx(out=wc[:].bitcast(FP8X4), scales=ws[:], in_=wg[:])
-
-        vg = const.tile([P, 2 * C * 4], BF16, name="vg", align_bytes=64)
-        bank = tps.tile([P, WORDS], F32, name="bank")
-        transpose_row_tile(vr[:].bitcast(F32), bank)
-        nc.vector.tensor_copy(
-            out=vg[:].bitcast(F32).rearrange("p (g c u) -> p g c u", g=2, c=C, u=2), in_=bank_view(bank)
-        )
+        t4 = prep.tile([P, D], F32, name="t4")
+        nc.vector.tensor_tensor(out=t4[:], in0=t3[:], in1=q4[:], op=ALU.subtract)
+        lb = prep.tile([P, D], F32, name="lb")
         vc = const.tile([P, 2 * C], U32, name="vc", align_bytes=64)
         vs = const.tile([P, 2 * C], U8, name="vs", align_bytes=64)
-        nc.vector.quantize_mx(out=vc[:].bitcast(FP8X4), scales=vs[:], in_=vg[:])
 
-        cbt = const.tile([P, C], F32, name="cbt")
-        nc.vector.tensor_copy(out=cbt[:], in_=cb16[:])
-        bbt = const.tile([P, C], F32, name="bbt")
-        nc.vector.tensor_copy(out=bbt[:], in_=bb16[:])
+        def softplus_ln():
+            nc.scalar.activation(out=lb[:], in_=u[:], func=ACT.Ln, scale=1.0, bias=1.0)
+            warm = prep.tile([P, 1], F32, name="warm")
+            nc.scalar.activation(out=warm[:], in_=u[:, 0:1], func=ACT.Abs_reciprocal_sqrt, scale=1.0, bias=1.0)
 
-        for q in range(NQ):
-            rows = slice(q * QROWS, (q + 1) * QROWS)
-            if q == 0:
-                xt = xts[0]
-            else:
-                xt = xin.tile([P, J * D], BF16, name="xt")
-                nc.sync.dma_start(out=xt[:], in_=x[rows, :].rearrange("(p j) k -> p (j k)", j=J))
-            xw = xt[:].bitcast(F32)
+        def softplus_end():
+            m1 = prep.tile([P, D], F32, name="m1")
+            nc.vector.tensor_tensor(out=m1[:], in0=t3[:], in1=lb[:], op=ALU.min)
+            m2 = prep.tile([P, D], F32, name="m2")
+            nc.vector.tensor_tensor(out=m2[:], in0=m1[:], in1=t4[:], op=ALU.max)
+            vr = prep.tile([P, D], BF16, name="vr")
+            nc.vector.scalar_tensor_tensor(out=vr[:], in0=sg[:], scalar=0.0, in1=m2[:], op0=ALU.max, op1=ALU.add)
+            vg = const.tile([P, 2 * C * 4], BF16, name="vg", align_bytes=64)
+            wbank = ops.tile([P, WORDS], F32, name="wbank")
+            transpose_row_tile(vr[:].bitcast(F32), wbank)
+            nc.vector.tensor_copy(
+                out=vg[:].bitcast(F32).rearrange("p (g c u) -> p g c u", g=2, c=C, u=2), in_=bank_view(wbank)
+            )
+            nc.vector.quantize_mx(out=vc[:].bitcast(FP8X4), scales=vs[:], in_=vg[:])
 
-            xg = grp.tile([P, J * D], BF16, name="xg", align_bytes=64)
-            xgw = xg[:].bitcast(F32).rearrange("p (j g r u) -> p j g r u", j=J, g=2, r=P, u=2)
-            banks = []
+        def st_t(q):
+            xw = xt[q][:].bitcast(F32)
+            banks[q] = []
             for j in range(J):
                 bank = tps.tile([P, WORDS], F32, name="bank")
                 transpose_row_tile(xw[:, j * WORDS:(j + 1) * WORDS], bank)
-                banks.append(bank)
+                banks[q].append(bank)
+
+        def st_c(q):
+            xg[q] = grp.tile([P, J * D], BF16, name="xg", align_bytes=64)
+            xgw = xg[q][:].bitcast(F32).rearrange("p (j g r u) -> p j g r u", j=J, g=2, r=P, u=2)
             for j in range(J):
-                nc.scalar.copy(out=xgw[:, j], in_=bank_view(banks[j]))
+                nc.scalar.copy(out=xgw[:, j], in_=bank_view(banks[q][j]))
+            sq[q] = grp.tile([P, J * D], BF16, name="sq", align_bytes=64)
 
-            sq = grp.tile([P, J * D], BF16, name="sq", align_bytes=64)
-            nc.vector.tensor_tensor(out=sq[:, :VSPLIT], in0=xg[:, :VSPLIT], in1=xg[:, :VSPLIT], op=ALU.mult)
-            nc.scalar.activation(out=sq[:, VSPLIT:], in_=xg[:, VSPLIT:], func=ACT.Square)
-
-            xc = cod.tile([P, J * 2 * P], U32, name="xc", align_bytes=64)
-            xs = cod.tile([P, J * 2 * P], U8, name="xs", align_bytes=64)
-            nc.vector.quantize_mx(out=xc[:].bitcast(FP8X4), scales=xs[:], in_=xg[:])
-            sc_ = cod.tile([P, J * 2 * P], U32, name="sc_", align_bytes=64)
-            ss = cod.tile([P, J * 2 * P], U8, name="ss", align_bytes=64)
-            nc.vector.quantize_mx(out=sc_[:].bitcast(FP8X4), scales=ss[:], in_=sq[:])
-
-            md = [mdp.tile([P, 512], F32, name="md") for h in range(2)]
-            for j in range(J):
-                for g in range(2):
-                    sl = slice((j * 2 + g) * P, (j * 2 + g + 1) * P)
-                    nc.tensor.matmul_mx(
-                        out=md[j // 2][:, (j % 2) * 256:(j % 2 + 1) * 256],
-                        lhsT=xc[:, sl].bitcast(FP8X4),
-                        lhsT_scale=xs[:, sl],
-                        rhs=wc[:, g * 256:(g + 1) * 256].bitcast(FP8X4),
-                        rhs_scale=ws[:, g * 256:(g + 1) * 256],
-                        start=(g == 0),
-                        stop=(g == 1),
-                    )
-            vb = vps.tile([P, 512], F32, name="vb")
-            for j in range(J):
-                for g in range(2):
-                    sl = slice((j * 2 + g) * P, (j * 2 + g + 1) * P)
-                    nc.tensor.matmul_mx(
-                        out=vb[:, j * C:(j + 1) * C],
-                        lhsT=sc_[:, sl].bitcast(FP8X4),
-                        lhsT_scale=ss[:, sl],
-                        rhs=vc[:, g * C:(g + 1) * C].bitcast(FP8X4),
-                        rhs_scale=vs[:, g * C:(g + 1) * C],
-                        start=(g == 0),
-                        stop=(g == 1),
-                    )
-
-            kk = epi.tile([P, J * C], F32, name="kk")
-            nc.scalar.activation(
-                out=kk[:], in_=vb[:], func=ACT.Abs_reciprocal_sqrt, scale=math.pi / 3200.0, bias=1.0 / 400.0
-            )
-            tm = epi.tile([P, J * C], F32, name="tm")
-            dl = res.tile([P, J * C], F32, name="dl")
-            so = res.tile([P, J * C], F32, name="so")
-            for h in range(2):
-                mdv = md[h][:].rearrange("p (t s c) -> p t s c", t=2, s=2, c=C)
-                hs = slice(h * 2 * C, (h + 1) * 2 * C)
-                nc.vector.tensor_tensor(
-                    out=dl[:, hs].rearrange("p (t c) -> p t c", t=2),
-                    in0=mdv[:, :, 1, :],
-                    in1=bbt[:].unsqueeze(1).to_broadcast([P, 2, C]),
-                    op=ALU.add,
-                )
-            nc.sync.dma_start(out=out_1[rows, :].rearrange("(p j) c -> p (j c)", j=J), in_=dl[:])
-            for h in range(2):
-                mdv = md[h][:].rearrange("p (t s c) -> p t s c", t=2, s=2, c=C)
-                hs = slice(h * 2 * C, (h + 1) * 2 * C)
-                nc.vector.tensor_tensor(
-                    out=tm[:, hs].rearrange("p (t c) -> p t c", t=2),
-                    in0=mdv[:, :, 0, :],
-                    in1=kk[:, hs].rearrange("p (t c) -> p t c", t=2),
-                    op=ALU.mult,
-                )
+        def st_qv(q):
             nc.vector.tensor_tensor(
+                out=sq[q][:, :VSPLIT], in0=xg[q][:, :VSPLIT], in1=xg[q][:, :VSPLIT], op=ALU.mult
+            )
+
+        def st_qs(q, lo, hi):
+            nc.scalar.activation(out=sq[q][:, lo:hi], in_=xg[q][:, lo:hi], func=ACT.Square)
+
+        def st_zx(q):
+            xc[q] = cod.tile([P, J * 2 * P], U32, name="xc", align_bytes=64)
+            xs[q] = cod.tile([P, J * 2 * P], U8, name="xs", align_bytes=64)
+            nc.vector.quantize_mx(out=xc[q][:].bitcast(FP8X4), scales=xs[q][:], in_=xg[q][:])
+
+        def st_zs(q):
+            qc[q] = cod.tile([P, J * 2 * P], U32, name="qc", align_bytes=64)
+            qs[q] = cod.tile([P, J * 2 * P], U8, name="qs", align_bytes=64)
+            nc.vector.quantize_mx(out=qc[q][:].bitcast(FP8X4), scales=qs[q][:], in_=sq[q][:])
+
+        def mx(out, codes, scales, sl, wcodes, wscales, wsl, g):
+            nc.tensor.matmul_mx(
+                out=out,
+                lhsT=codes[:, sl].bitcast(FP8X4),
+                lhsT_scale=scales[:, sl],
+                rhs=wcodes[:, wsl].bitcast(FP8X4),
+                rhs_scale=wscales[:, wsl],
+                start=(g == 0),
+                stop=(g == 1),
+            )
+
+        def st_md(q):
+            mb[q] = ops.tile([P, J * C], F32, name="mb")
+            db[q] = ops.tile([P, J * C], F32, name="db")
+            for j in range(J):
+                for g in range(2):
+                    sl = slice((j * 2 + g) * P, (j * 2 + g + 1) * P)
+                    mx(mb[q][:, j * C:(j + 1) * C], xc[q], xs[q], sl, wc, ws, slice(g * C, (g + 1) * C), g)
+                    mx(db[q][:, j * C:(j + 1) * C], xc[q], xs[q], sl, wc, ws, slice((2 + g) * C, (3 + g) * C), g)
+
+        def st_vv(q):
+            vb[q] = ops.tile([P, J * C], F32, name="vb")
+            for j in range(J):
+                for g in range(2):
+                    sl = slice((j * 2 + g) * P, (j * 2 + g + 1) * P)
+                    mx(vb[q][:, j * C:(j + 1) * C], qc[q], qs[q], sl, vc, vs, slice(g * C, (g + 1) * C), g)
+
+        def st_k(q):
+            kk[q] = epi.tile([P, J * C], F32, name="kk")
+            nc.scalar.activation(
+                out=kk[q][:], in_=vb[q][:], func=ACT.Abs_reciprocal_sqrt, scale=math.pi / 3200.0, bias=1.0 / 400.0
+            )
+
+        def st_e1(q):
+            dl = res.tile([P, J * C], F32, name="dl")
+            nc.vector.tensor_tensor(
+                out=dl[:].rearrange("p (t c) -> p t c", t=J),
+                in0=db[q][:].rearrange("p (t c) -> p t c", t=J),
+                in1=bbt[:].unsqueeze(1).to_broadcast([P, J, C]),
+                op=ALU.add,
+            )
+            nc.sync.dma_start(
+                out=out_1[q * QROWS:(q + 1) * QROWS, :].rearrange("(p j) c -> p (j c)", j=J), in_=dl[:]
+            )
+
+        def st_e2(q):
+            tm[q] = epi.tile([P, J * C], F32, name="tm")
+            nc.vector.tensor_tensor(out=tm[q][:], in0=mb[q][:], in1=kk[q][:], op=ALU.mult)
+
+        def st_e3(q):
+            so = res.tile([P, J * C], F32, name="so")
+            eng = nc.vector if (False or (True and q == NQ - 1)) else nc.gpsimd
+            eng.tensor_tensor(
                 out=so[:].rearrange("p (t c) -> p t c", t=J),
-                in0=tm[:].rearrange("p (t c) -> p t c", t=J),
+                in0=tm[q][:].rearrange("p (t c) -> p t c", t=J),
                 in1=cbt[:].unsqueeze(1).to_broadcast([P, J, C]),
                 op=ALU.add,
             )
-            nc.sync.dma_start(out=out_0[rows, :].rearrange("(p j) c -> p (j c)", j=J), in_=so[:])
+            nc.sync.dma_start(
+                out=out_0[q * QROWS:(q + 1) * QROWS, :].rearrange("(p j) c -> p (j c)", j=J), in_=so[:]
+            )
+
+        def ok(q):
+            return 0 <= q < NQ
+
+        for t in range(-2, NQ + 1):
+            if PRE - 2 <= t + PRE < NQ:
+                load(t + PRE)
+            if ok(t - 1):
+                st_e2(t - 1)
+                st_e3(t - 1)
+            if ok(t):
+                st_md(t)
+            if t == 0:
+                softplus_end()
+            if ok(t):
+                st_zs(t)
+                st_vv(t)
+            if ok(t + 1):
+                st_c(t + 1)
+            if t == -1:
+                softplus_ln()
+            if ok(t + 2):
+                st_t(t + 2)
+            if ok(t + 1):
+                st_qv(t + 1)
+                st_qs(t + 1, VSPLIT, VSPLIT + QSA)
+            if ok(t):
+                st_k(t)
+            if ok(t + 1):
+                st_qs(t + 1, VSPLIT + QSA, J * D)
+                st_zx(t + 1)
+            if ok(t):
+                st_e1(t)

@@ -140,10 +140,11 @@ def tile_bayesianoutputlayers_t_kernel(tc, x, cls_w, cls_b, sigma_w, bbox_w, bbo
             )
             nc.vector.quantize_mx(out=vc[:].bitcast(FP8X4), scales=vs[:], in_=vg[:])
 
-        def st_t(q):
+        def st_t(q, half):
             xw = xt[q][:].bitcast(F32)
-            banks[q] = []
-            for j in range(J):
+            if half == 0:
+                banks[q] = []
+            for j in range(2 * half, 2 * half + 2):
                 bank = tps.tile([P, WORDS], F32, name="bank")
                 transpose_row_tile(xw[:, j * WORDS:(j + 1) * WORDS], bank)
                 banks[q].append(bank)
@@ -184,14 +185,32 @@ def tile_bayesianoutputlayers_t_kernel(tc, x, cls_w, cls_b, sigma_w, bbox_w, bbo
                 stop=(g == 1),
             )
 
-        def st_md(q):
-            mb[q] = ops.tile([P, J * C], F32, name="mb")
+        def st_d(q):
             db[q] = ops.tile([P, J * C], F32, name="db")
             for j in range(J):
                 for g in range(2):
                     sl = slice((j * 2 + g) * P, (j * 2 + g + 1) * P)
-                    mx(mb[q][:, j * C:(j + 1) * C], xc[q], xs[q], sl, wc, ws, slice(g * C, (g + 1) * C), g)
                     mx(db[q][:, j * C:(j + 1) * C], xc[q], xs[q], sl, wc, ws, slice((2 + g) * C, (3 + g) * C), g)
+
+        def st_m(q):
+            mb[q] = ops.tile([P, J * C], F32, name="mb")
+            for j in range(J):
+                for g in range(2):
+                    sl = slice((j * 2 + g) * P, (j * 2 + g + 1) * P)
+                    mx(mb[q][:, j * C:(j + 1) * C], xc[q], xs[q], sl, wc, ws, slice(g * C, (g + 1) * C), g)
+
+        def st_dummy(n):
+            idle = ops.tile([P, 512], F32, name="wbank")
+            for i in range(n):
+                nc.tensor.matmul_mx(
+                    out=idle[:],
+                    lhsT=wc[:, 0:P].bitcast(FP8X4),
+                    lhsT_scale=ws[:, 0:P],
+                    rhs=wc[:].bitcast(FP8X4),
+                    rhs_scale=ws[:],
+                    start=True,
+                    stop=True,
+                )
 
         def st_vv(q):
             vb[q] = ops.tile([P, J * C], F32, name="vb")
@@ -241,22 +260,29 @@ def tile_bayesianoutputlayers_t_kernel(tc, x, cls_w, cls_b, sigma_w, bbox_w, bbo
         for t in range(-2, NQ + 1):
             if PRE - 2 <= t + PRE < NQ:
                 load(t + PRE)
+            if ok(t):
+                st_d(t)
             if ok(t - 1):
                 st_e2(t - 1)
                 st_e3(t - 1)
             if ok(t):
-                st_md(t)
+                st_m(t)
             if t == 0:
                 softplus_end()
             if ok(t):
                 st_zs(t)
-                st_vv(t)
             if ok(t + 1):
                 st_c(t + 1)
             if t == -1:
                 softplus_ln()
             if ok(t + 2):
-                st_t(t + 2)
+                st_t(t + 2, 0)
+            if ok(t):
+                st_vv(t)
+            if ok(t + 2):
+                st_t(t + 2, 1)
+            if 1 <= t < NQ - 1 and 2 > 0:
+                st_dummy(2)
             if ok(t + 1):
                 st_qv(t + 1)
                 st_qs(t + 1, VSPLIT, VSPLIT + QSA)

@@ -10,6 +10,7 @@ F32 = mybir.dt.float32
 BF16 = mybir.dt.bfloat16
 U32 = mybir.dt.uint32
 U8 = mybir.dt.uint8
+I32 = mybir.dt.int32
 FP8X4 = mybir.dt.float8_e4m3fn_x4
 ACT = mybir.ActivationFunctionType
 ALU = mybir.AluOpType
@@ -22,7 +23,7 @@ QROWS = P * J
 NQ = 16
 C = 128
 VSPLIT = 2304
-QSA = 896
+SIGN_BITS = -2147450880
 PRE = 5
 
 
@@ -91,19 +92,21 @@ def tile_bayesianoutputlayers_t_kernel(tc, x, cls_w, cls_b, sigma_w, bbox_w, bbo
         def bank_view(bank):
             return bank[:].rearrange("p (g u r) -> p g r u", g=2, u=2, r=P)
 
-        ab = prep.tile([P, D], F32, name="ab")
-        nc.scalar.activation(out=ab[:], in_=sg[:], func=ACT.Abs)
+        na = prep.tile([P, D], BF16, name="na")
+        nc.vector.tensor_single_scalar(
+            out=na[:].bitcast(I32), in_=sg[:].bitcast(I32), scalar=SIGN_BITS, op=ALU.bitwise_or
+        )
         u = prep.tile([P, D], F32, name="u")
-        nc.scalar.activation(out=u[:], in_=ab[:], func=ACT.Exp, scale=-1.0)
+        nc.scalar.activation(out=u[:], in_=na[:], func=ACT.Exp)
 
         wg = const.tile([P, 2 * 2 * C * 4], BF16, name="wg", align_bytes=64)
         wgw = wg[:].bitcast(F32).rearrange("p (w g c u) -> p w g c u", w=2, g=2, c=C, u=2)
-        for w, src in enumerate((cw, bw)):
-            wbank = ops.tile([P, WORDS], F32, name="wbank")
+        for w, src, tag in ((0, cw, "mb"), (1, bw, "db")):
+            wbank = ops.tile([P, WORDS], F32, name=tag)
             transpose_row_tile(src[:].bitcast(F32), wbank)
             nc.scalar.copy(out=wgw[:, w], in_=bank_view(wbank))
         q4 = prep.tile([P, D], F32, name="q4")
-        nc.scalar.activation(out=q4[:], in_=ab[:], func=ACT.Exp, scale=-4.0, bias=1.0e-6 - math.log(4.0))
+        nc.scalar.activation(out=q4[:], in_=na[:], func=ACT.Exp, scale=4.0, bias=1.0e-6 - math.log(4.0))
 
         a1 = prep.tile([P, D], F32, name="a1")
         nc.vector.tensor_scalar(out=a1[:], in0=u[:], scalar1=1.0 / 3.0, scalar2=-0.5, op0=ALU.mult, op1=ALU.add)
@@ -285,11 +288,10 @@ def tile_bayesianoutputlayers_t_kernel(tc, x, cls_w, cls_b, sigma_w, bbox_w, bbo
                 st_dummy(2)
             if ok(t + 1):
                 st_qv(t + 1)
-                st_qs(t + 1, VSPLIT, VSPLIT + QSA)
+                st_qs(t + 1, VSPLIT, J * D)
             if ok(t):
                 st_k(t)
             if ok(t + 1):
-                st_qs(t + 1, VSPLIT + QSA, J * D)
                 st_zx(t + 1)
             if ok(t):
                 st_e1(t)

@@ -20,11 +20,12 @@ D = 1024
 WORDS = D // 2
 J = 4
 QROWS = P * J
-NQ = 16
+NQ = 8192 // QROWS
 C = 128
 VSPLIT = 2304
 SIGN_BITS = -2147450880
 PRE = 5
+IDLE_PASSES = 2
 
 
 def tile_bayesianoutputlayers_t_kernel(tc, x, cls_w, cls_b, sigma_w, bbox_w, bbox_b, out_0, out_1):
@@ -98,15 +99,17 @@ def tile_bayesianoutputlayers_t_kernel(tc, x, cls_w, cls_b, sigma_w, bbox_w, bbo
         )
         u = prep.tile([P, D], F32, name="u")
         nc.scalar.activation(out=u[:], in_=na[:], func=ACT.Exp)
+        q4 = prep.tile([P, D], F32, name="q4")
+        nc.scalar.activation(out=q4[:], in_=na[:], func=ACT.Exp, scale=4.0, bias=1.0e-6 - math.log(4.0))
+        lb = prep.tile([P, D], F32, name="lb")
+        nc.scalar.activation(out=lb[:], in_=u[:], func=ACT.Ln, scale=1.0, bias=1.0)
 
         wg = const.tile([P, 2 * 2 * C * 4], BF16, name="wg", align_bytes=64)
         wgw = wg[:].bitcast(F32).rearrange("p (w g c u) -> p w g c u", w=2, g=2, c=C, u=2)
         for w, src, tag in ((0, cw, "mb"), (1, bw, "db")):
             wbank = ops.tile([P, WORDS], F32, name=tag)
             transpose_row_tile(src[:].bitcast(F32), wbank)
-            nc.scalar.copy(out=wgw[:, w], in_=bank_view(wbank))
-        q4 = prep.tile([P, D], F32, name="q4")
-        nc.scalar.activation(out=q4[:], in_=na[:], func=ACT.Exp, scale=4.0, bias=1.0e-6 - math.log(4.0))
+            nc.vector.tensor_copy(out=wgw[:, w], in_=bank_view(wbank))
 
         a1 = prep.tile([P, D], F32, name="a1")
         nc.vector.tensor_scalar(out=a1[:], in0=u[:], scalar1=1.0 / 3.0, scalar2=-0.5, op0=ALU.mult, op1=ALU.add)
@@ -114,27 +117,21 @@ def tile_bayesianoutputlayers_t_kernel(tc, x, cls_w, cls_b, sigma_w, bbox_w, bbo
         nc.vector.tensor_tensor(out=a2[:], in0=a1[:], in1=u[:], op=ALU.mult)
         t3 = prep.tile([P, D], F32, name="t3")
         nc.vector.scalar_tensor_tensor(out=t3[:], in0=a2[:], scalar=1.0, in1=u[:], op0=ALU.add, op1=ALU.mult)
+        t4 = prep.tile([P, D], F32, name="t4")
+        nc.vector.tensor_tensor(out=t4[:], in0=t3[:], in1=q4[:], op=ALU.subtract)
+        m1 = prep.tile([P, D], F32, name="m1")
+        nc.vector.tensor_tensor(out=m1[:], in0=t3[:], in1=lb[:], op=ALU.min)
+        m2 = prep.tile([P, D], F32, name="m2")
+        nc.vector.tensor_tensor(out=m2[:], in0=m1[:], in1=t4[:], op=ALU.max)
+        vr = prep.tile([P, D], BF16, name="vr")
+        nc.vector.scalar_tensor_tensor(out=vr[:], in0=sg[:], scalar=0.0, in1=m2[:], op0=ALU.max, op1=ALU.add)
         wc = const.tile([P, 2 * 2 * C], U32, name="wc", align_bytes=64)
         ws = const.tile([P, 2 * 2 * C], U8, name="ws", align_bytes=64)
         nc.vector.quantize_mx(out=wc[:].bitcast(FP8X4), scales=ws[:], in_=wg[:])
-        t4 = prep.tile([P, D], F32, name="t4")
-        nc.vector.tensor_tensor(out=t4[:], in0=t3[:], in1=q4[:], op=ALU.subtract)
-        lb = prep.tile([P, D], F32, name="lb")
         vc = const.tile([P, 2 * C], U32, name="vc", align_bytes=64)
         vs = const.tile([P, 2 * C], U8, name="vs", align_bytes=64)
 
-        def softplus_ln():
-            nc.scalar.activation(out=lb[:], in_=u[:], func=ACT.Ln, scale=1.0, bias=1.0)
-            warm = prep.tile([P, 1], F32, name="warm")
-            nc.scalar.activation(out=warm[:], in_=u[:, 0:1], func=ACT.Abs_reciprocal_sqrt, scale=1.0, bias=1.0)
-
-        def softplus_end():
-            m1 = prep.tile([P, D], F32, name="m1")
-            nc.vector.tensor_tensor(out=m1[:], in0=t3[:], in1=lb[:], op=ALU.min)
-            m2 = prep.tile([P, D], F32, name="m2")
-            nc.vector.tensor_tensor(out=m2[:], in0=m1[:], in1=t4[:], op=ALU.max)
-            vr = prep.tile([P, D], BF16, name="vr")
-            nc.vector.scalar_tensor_tensor(out=vr[:], in0=sg[:], scalar=0.0, in1=m2[:], op0=ALU.max, op1=ALU.add)
+        def var_codes():
             vg = const.tile([P, 2 * C * 4], BF16, name="vg", align_bytes=64)
             wbank = ops.tile([P, WORDS], F32, name="wbank")
             transpose_row_tile(vr[:].bitcast(F32), wbank)
@@ -142,6 +139,10 @@ def tile_bayesianoutputlayers_t_kernel(tc, x, cls_w, cls_b, sigma_w, bbox_w, bbo
                 out=vg[:].bitcast(F32).rearrange("p (g c u) -> p g c u", g=2, c=C, u=2), in_=bank_view(wbank)
             )
             nc.vector.quantize_mx(out=vc[:].bitcast(FP8X4), scales=vs[:], in_=vg[:])
+
+        def load_k_table():
+            warm = prep.tile([P, 1], F32, name="warm")
+            nc.scalar.activation(out=warm[:], in_=u[:, 0:1], func=ACT.Abs_reciprocal_sqrt, scale=1.0, bias=1.0)
 
         def st_t(q, half):
             xw = xt[q][:].bitcast(F32)
@@ -164,8 +165,8 @@ def tile_bayesianoutputlayers_t_kernel(tc, x, cls_w, cls_b, sigma_w, bbox_w, bbo
                 out=sq[q][:, :VSPLIT], in0=xg[q][:, :VSPLIT], in1=xg[q][:, :VSPLIT], op=ALU.mult
             )
 
-        def st_qs(q, lo, hi):
-            nc.scalar.activation(out=sq[q][:, lo:hi], in_=xg[q][:, lo:hi], func=ACT.Square)
+        def st_qs(q):
+            nc.scalar.activation(out=sq[q][:, VSPLIT:], in_=xg[q][:, VSPLIT:], func=ACT.Square)
 
         def st_zx(q):
             xc[q] = cod.tile([P, J * 2 * P], U32, name="xc", align_bytes=64)
@@ -177,34 +178,36 @@ def tile_bayesianoutputlayers_t_kernel(tc, x, cls_w, cls_b, sigma_w, bbox_w, bbo
             qs[q] = cod.tile([P, J * 2 * P], U8, name="qs", align_bytes=64)
             nc.vector.quantize_mx(out=qc[q][:].bitcast(FP8X4), scales=qs[q][:], in_=sq[q][:])
 
-        def mx(out, codes, scales, sl, wcodes, wscales, wsl, g):
-            nc.tensor.matmul_mx(
-                out=out,
-                lhsT=codes[:, sl].bitcast(FP8X4),
-                lhsT_scale=scales[:, sl],
-                rhs=wcodes[:, wsl].bitcast(FP8X4),
-                rhs_scale=wscales[:, wsl],
-                start=(g == 0),
-                stop=(g == 1),
-            )
+        def passes(bank, codes, scales, wcodes, wscales, first):
+            for j in range(J):
+                for g in range(2):
+                    sl = slice((j * 2 + g) * P, (j * 2 + g + 1) * P)
+                    wsl = slice((first + g) * C, (first + g + 1) * C)
+                    nc.tensor.matmul_mx(
+                        out=bank[:, j * C:(j + 1) * C],
+                        lhsT=codes[:, sl].bitcast(FP8X4),
+                        lhsT_scale=scales[:, sl],
+                        rhs=wcodes[:, wsl].bitcast(FP8X4),
+                        rhs_scale=wscales[:, wsl],
+                        start=(g == 0),
+                        stop=(g == 1),
+                    )
 
         def st_d(q):
             db[q] = ops.tile([P, J * C], F32, name="db")
-            for j in range(J):
-                for g in range(2):
-                    sl = slice((j * 2 + g) * P, (j * 2 + g + 1) * P)
-                    mx(db[q][:, j * C:(j + 1) * C], xc[q], xs[q], sl, wc, ws, slice((2 + g) * C, (3 + g) * C), g)
+            passes(db[q], xc[q], xs[q], wc, ws, 2)
 
         def st_m(q):
             mb[q] = ops.tile([P, J * C], F32, name="mb")
-            for j in range(J):
-                for g in range(2):
-                    sl = slice((j * 2 + g) * P, (j * 2 + g + 1) * P)
-                    mx(mb[q][:, j * C:(j + 1) * C], xc[q], xs[q], sl, wc, ws, slice(g * C, (g + 1) * C), g)
+            passes(mb[q], xc[q], xs[q], wc, ws, 0)
 
-        def st_dummy(n):
+        def st_vv(q):
+            vb[q] = ops.tile([P, J * C], F32, name="vb")
+            passes(vb[q], qc[q], qs[q], vc, vs, 0)
+
+        def st_idle():
             idle = ops.tile([P, 512], F32, name="wbank")
-            for i in range(n):
+            for i in range(IDLE_PASSES):
                 nc.tensor.matmul_mx(
                     out=idle[:],
                     lhsT=wc[:, 0:P].bitcast(FP8X4),
@@ -214,13 +217,6 @@ def tile_bayesianoutputlayers_t_kernel(tc, x, cls_w, cls_b, sigma_w, bbox_w, bbo
                     start=True,
                     stop=True,
                 )
-
-        def st_vv(q):
-            vb[q] = ops.tile([P, J * C], F32, name="vb")
-            for j in range(J):
-                for g in range(2):
-                    sl = slice((j * 2 + g) * P, (j * 2 + g + 1) * P)
-                    mx(vb[q][:, j * C:(j + 1) * C], qc[q], qs[q], sl, vc, vs, slice(g * C, (g + 1) * C), g)
 
         def st_k(q):
             kk[q] = epi.tile([P, J * C], F32, name="kk")
@@ -244,9 +240,11 @@ def tile_bayesianoutputlayers_t_kernel(tc, x, cls_w, cls_b, sigma_w, bbox_w, bbo
             tm[q] = epi.tile([P, J * C], F32, name="tm")
             nc.vector.tensor_tensor(out=tm[q][:], in0=mb[q][:], in1=kk[q][:], op=ALU.mult)
 
-        def st_e3(q):
+        def st_e3(q, gate):
             so = res.tile([P, J * C], F32, name="so")
-            eng = nc.vector if (False or (True and q == NQ - 1)) else nc.gpsimd
+            eng = nc.vector if q == NQ - 1 else nc.gpsimd
+            if gate is not None:
+                nc.gpsimd.tensor_copy(out=token[:], in_=gate[:, 0:1])
             eng.tensor_tensor(
                 out=so[:].rearrange("p (t c) -> p t c", t=J),
                 in0=tm[q][:].rearrange("p (t c) -> p t c", t=J),
@@ -257,38 +255,47 @@ def tile_bayesianoutputlayers_t_kernel(tc, x, cls_w, cls_b, sigma_w, bbox_w, bbo
                 out=out_0[q * QROWS:(q + 1) * QROWS, :].rearrange("(p j) c -> p (j c)", j=J), in_=so[:]
             )
 
+        token = prep.tile([P, 1], BF16, name="token")
+
         def ok(q):
             return 0 <= q < NQ
 
         for t in range(-2, NQ + 1):
+            last = t == NQ - 1
             if PRE - 2 <= t + PRE < NQ:
                 load(t + PRE)
             if ok(t):
                 st_d(t)
+            if last:
+                st_zs(t)
+                st_vv(t)
             if ok(t - 1):
                 st_e2(t - 1)
-                st_e3(t - 1)
+                if not ok(t + 1):
+                    st_e3(t - 1, None)
             if ok(t):
                 st_m(t)
-            if t == 0:
-                softplus_end()
-            if ok(t):
+            if ok(t) and not last:
                 st_zs(t)
             if ok(t + 1):
                 st_c(t + 1)
-            if t == -1:
-                softplus_ln()
             if ok(t + 2):
                 st_t(t + 2, 0)
-            if ok(t):
+            if ok(t) and not last:
                 st_vv(t)
             if ok(t + 2):
                 st_t(t + 2, 1)
-            if 1 <= t < NQ - 1 and 2 > 0:
-                st_dummy(2)
+            if 0 <= t < NQ - 1:
+                st_idle()
             if ok(t + 1):
                 st_qv(t + 1)
-                st_qs(t + 1, VSPLIT, J * D)
+                if ok(t - 1):
+                    st_e3(t - 1, sq[t + 1])
+                st_qs(t + 1)
+            if t == -1:
+                var_codes()
+            if t == 0:
+                load_k_table()
             if ok(t):
                 st_k(t)
             if ok(t + 1):

@@ -20,12 +20,11 @@ D = 1024
 WORDS = D // 2
 J = 4
 QROWS = P * J
-NQ = 8192 // QROWS
+NQ = 16
 C = 128
-VSPLIT = 2304
+VSPLIT = 2112
 SIGN_BITS = -2147450880
 PRE = 5
-IDLE_PASSES = 2
 
 
 def tile_bayesianoutputlayers_t_kernel(tc, x, cls_w, cls_b, sigma_w, bbox_w, bbox_b, out_0, out_1):
@@ -99,17 +98,15 @@ def tile_bayesianoutputlayers_t_kernel(tc, x, cls_w, cls_b, sigma_w, bbox_w, bbo
         )
         u = prep.tile([P, D], F32, name="u")
         nc.scalar.activation(out=u[:], in_=na[:], func=ACT.Exp)
-        q4 = prep.tile([P, D], F32, name="q4")
-        nc.scalar.activation(out=q4[:], in_=na[:], func=ACT.Exp, scale=4.0, bias=1.0e-6 - math.log(4.0))
-        lb = prep.tile([P, D], F32, name="lb")
-        nc.scalar.activation(out=lb[:], in_=u[:], func=ACT.Ln, scale=1.0, bias=1.0)
 
         wg = const.tile([P, 2 * 2 * C * 4], BF16, name="wg", align_bytes=64)
         wgw = wg[:].bitcast(F32).rearrange("p (w g c u) -> p w g c u", w=2, g=2, c=C, u=2)
         for w, src, tag in ((0, cw, "mb"), (1, bw, "db")):
             wbank = ops.tile([P, WORDS], F32, name=tag)
             transpose_row_tile(src[:].bitcast(F32), wbank)
-            nc.vector.tensor_copy(out=wgw[:, w], in_=bank_view(wbank))
+            nc.scalar.copy(out=wgw[:, w], in_=bank_view(wbank))
+        q4 = prep.tile([P, D], F32, name="q4")
+        nc.scalar.activation(out=q4[:], in_=na[:], func=ACT.Exp, scale=4.0, bias=1.0e-6 - math.log(4.0))
 
         a1 = prep.tile([P, D], F32, name="a1")
         nc.vector.tensor_scalar(out=a1[:], in0=u[:], scalar1=1.0 / 3.0, scalar2=-0.5, op0=ALU.mult, op1=ALU.add)
@@ -117,21 +114,27 @@ def tile_bayesianoutputlayers_t_kernel(tc, x, cls_w, cls_b, sigma_w, bbox_w, bbo
         nc.vector.tensor_tensor(out=a2[:], in0=a1[:], in1=u[:], op=ALU.mult)
         t3 = prep.tile([P, D], F32, name="t3")
         nc.vector.scalar_tensor_tensor(out=t3[:], in0=a2[:], scalar=1.0, in1=u[:], op0=ALU.add, op1=ALU.mult)
-        t4 = prep.tile([P, D], F32, name="t4")
-        nc.vector.tensor_tensor(out=t4[:], in0=t3[:], in1=q4[:], op=ALU.subtract)
-        m1 = prep.tile([P, D], F32, name="m1")
-        nc.vector.tensor_tensor(out=m1[:], in0=t3[:], in1=lb[:], op=ALU.min)
-        m2 = prep.tile([P, D], F32, name="m2")
-        nc.vector.tensor_tensor(out=m2[:], in0=m1[:], in1=t4[:], op=ALU.max)
-        vr = prep.tile([P, D], BF16, name="vr")
-        nc.vector.scalar_tensor_tensor(out=vr[:], in0=sg[:], scalar=0.0, in1=m2[:], op0=ALU.max, op1=ALU.add)
         wc = const.tile([P, 2 * 2 * C], U32, name="wc", align_bytes=64)
         ws = const.tile([P, 2 * 2 * C], U8, name="ws", align_bytes=64)
         nc.vector.quantize_mx(out=wc[:].bitcast(FP8X4), scales=ws[:], in_=wg[:])
+        t4 = prep.tile([P, D], F32, name="t4")
+        nc.vector.tensor_tensor(out=t4[:], in0=t3[:], in1=q4[:], op=ALU.subtract)
+        lb = prep.tile([P, D], F32, name="lb")
         vc = const.tile([P, 2 * C], U32, name="vc", align_bytes=64)
         vs = const.tile([P, 2 * C], U8, name="vs", align_bytes=64)
 
-        def var_codes():
+        def softplus_ln():
+            nc.scalar.activation(out=lb[:], in_=u[:], func=ACT.Ln, scale=1.0, bias=1.0)
+            warm = prep.tile([P, 1], F32, name="warm")
+            nc.scalar.activation(out=warm[:], in_=u[:, 0:1], func=ACT.Abs_reciprocal_sqrt, scale=1.0, bias=1.0)
+
+        def softplus_end():
+            m1 = prep.tile([P, D], F32, name="m1")
+            nc.vector.tensor_tensor(out=m1[:], in0=t3[:], in1=lb[:], op=ALU.min)
+            m2 = prep.tile([P, D], F32, name="m2")
+            nc.vector.tensor_tensor(out=m2[:], in0=m1[:], in1=t4[:], op=ALU.max)
+            vr = prep.tile([P, D], BF16, name="vr")
+            nc.vector.scalar_tensor_tensor(out=vr[:], in0=sg[:], scalar=0.0, in1=m2[:], op0=ALU.max, op1=ALU.add)
             vg = const.tile([P, 2 * C * 4], BF16, name="vg", align_bytes=64)
             wbank = ops.tile([P, WORDS], F32, name="wbank")
             transpose_row_tile(vr[:].bitcast(F32), wbank)
@@ -139,10 +142,6 @@ def tile_bayesianoutputlayers_t_kernel(tc, x, cls_w, cls_b, sigma_w, bbox_w, bbo
                 out=vg[:].bitcast(F32).rearrange("p (g c u) -> p g c u", g=2, c=C, u=2), in_=bank_view(wbank)
             )
             nc.vector.quantize_mx(out=vc[:].bitcast(FP8X4), scales=vs[:], in_=vg[:])
-
-        def load_k_table():
-            warm = prep.tile([P, 1], F32, name="warm")
-            nc.scalar.activation(out=warm[:], in_=u[:, 0:1], func=ACT.Abs_reciprocal_sqrt, scale=1.0, bias=1.0)
 
         def st_t(q, half):
             xw = xt[q][:].bitcast(F32)
@@ -165,8 +164,8 @@ def tile_bayesianoutputlayers_t_kernel(tc, x, cls_w, cls_b, sigma_w, bbox_w, bbo
                 out=sq[q][:, :VSPLIT], in0=xg[q][:, :VSPLIT], in1=xg[q][:, :VSPLIT], op=ALU.mult
             )
 
-        def st_qs(q):
-            nc.scalar.activation(out=sq[q][:, VSPLIT:], in_=xg[q][:, VSPLIT:], func=ACT.Square)
+        def st_qs(q, lo, hi):
+            nc.scalar.activation(out=sq[q][:, lo:hi], in_=xg[q][:, lo:hi], func=ACT.Square)
 
         def st_zx(q):
             xc[q] = cod.tile([P, J * 2 * P], U32, name="xc", align_bytes=64)
@@ -178,36 +177,34 @@ def tile_bayesianoutputlayers_t_kernel(tc, x, cls_w, cls_b, sigma_w, bbox_w, bbo
             qs[q] = cod.tile([P, J * 2 * P], U8, name="qs", align_bytes=64)
             nc.vector.quantize_mx(out=qc[q][:].bitcast(FP8X4), scales=qs[q][:], in_=sq[q][:])
 
-        def passes(bank, codes, scales, wcodes, wscales, first):
-            for j in range(J):
-                for g in range(2):
-                    sl = slice((j * 2 + g) * P, (j * 2 + g + 1) * P)
-                    wsl = slice((first + g) * C, (first + g + 1) * C)
-                    nc.tensor.matmul_mx(
-                        out=bank[:, j * C:(j + 1) * C],
-                        lhsT=codes[:, sl].bitcast(FP8X4),
-                        lhsT_scale=scales[:, sl],
-                        rhs=wcodes[:, wsl].bitcast(FP8X4),
-                        rhs_scale=wscales[:, wsl],
-                        start=(g == 0),
-                        stop=(g == 1),
-                    )
+        def mx(out, codes, scales, sl, wcodes, wscales, wsl, g):
+            nc.tensor.matmul_mx(
+                out=out,
+                lhsT=codes[:, sl].bitcast(FP8X4),
+                lhsT_scale=scales[:, sl],
+                rhs=wcodes[:, wsl].bitcast(FP8X4),
+                rhs_scale=wscales[:, wsl],
+                start=(g == 0),
+                stop=(g == 1),
+            )
 
         def st_d(q):
             db[q] = ops.tile([P, J * C], F32, name="db")
-            passes(db[q], xc[q], xs[q], wc, ws, 2)
+            for j in range(J):
+                for g in range(2):
+                    sl = slice((j * 2 + g) * P, (j * 2 + g + 1) * P)
+                    mx(db[q][:, j * C:(j + 1) * C], xc[q], xs[q], sl, wc, ws, slice((2 + g) * C, (3 + g) * C), g)
 
         def st_m(q):
             mb[q] = ops.tile([P, J * C], F32, name="mb")
-            passes(mb[q], xc[q], xs[q], wc, ws, 0)
+            for j in range(J):
+                for g in range(2):
+                    sl = slice((j * 2 + g) * P, (j * 2 + g + 1) * P)
+                    mx(mb[q][:, j * C:(j + 1) * C], xc[q], xs[q], sl, wc, ws, slice(g * C, (g + 1) * C), g)
 
-        def st_vv(q):
-            vb[q] = ops.tile([P, J * C], F32, name="vb")
-            passes(vb[q], qc[q], qs[q], vc, vs, 0)
-
-        def st_idle():
+        def st_dummy(n):
             idle = ops.tile([P, 512], F32, name="wbank")
-            for i in range(IDLE_PASSES):
+            for i in range(n):
                 nc.tensor.matmul_mx(
                     out=idle[:],
                     lhsT=wc[:, 0:P].bitcast(FP8X4),
@@ -217,6 +214,13 @@ def tile_bayesianoutputlayers_t_kernel(tc, x, cls_w, cls_b, sigma_w, bbox_w, bbo
                     start=True,
                     stop=True,
                 )
+
+        def st_vv(q):
+            vb[q] = ops.tile([P, J * C], F32, name="vb")
+            for j in range(J):
+                for g in range(2):
+                    sl = slice((j * 2 + g) * P, (j * 2 + g + 1) * P)
+                    mx(vb[q][:, j * C:(j + 1) * C], qc[q], qs[q], sl, vc, vs, slice(g * C, (g + 1) * C), g)
 
         def st_k(q):
             kk[q] = epi.tile([P, J * C], F32, name="kk")
@@ -240,11 +244,9 @@ def tile_bayesianoutputlayers_t_kernel(tc, x, cls_w, cls_b, sigma_w, bbox_w, bbo
             tm[q] = epi.tile([P, J * C], F32, name="tm")
             nc.vector.tensor_tensor(out=tm[q][:], in0=mb[q][:], in1=kk[q][:], op=ALU.mult)
 
-        def st_e3(q, gate):
+        def st_e3(q):
             so = res.tile([P, J * C], F32, name="so")
-            eng = nc.vector if q == NQ - 1 else nc.gpsimd
-            if gate is not None:
-                nc.gpsimd.tensor_copy(out=token[:], in_=gate[:, 0:1])
+            eng = nc.vector if (False or (True and q == NQ - 1)) else nc.gpsimd
             eng.tensor_tensor(
                 out=so[:].rearrange("p (t c) -> p t c", t=J),
                 in0=tm[q][:].rearrange("p (t c) -> p t c", t=J),
@@ -255,47 +257,38 @@ def tile_bayesianoutputlayers_t_kernel(tc, x, cls_w, cls_b, sigma_w, bbox_w, bbo
                 out=out_0[q * QROWS:(q + 1) * QROWS, :].rearrange("(p j) c -> p (j c)", j=J), in_=so[:]
             )
 
-        token = prep.tile([P, 1], BF16, name="token")
-
         def ok(q):
             return 0 <= q < NQ
 
         for t in range(-2, NQ + 1):
-            last = t == NQ - 1
             if PRE - 2 <= t + PRE < NQ:
                 load(t + PRE)
             if ok(t):
                 st_d(t)
-            if last:
-                st_zs(t)
-                st_vv(t)
             if ok(t - 1):
                 st_e2(t - 1)
-                if not ok(t + 1):
-                    st_e3(t - 1, None)
+                st_e3(t - 1)
             if ok(t):
                 st_m(t)
-            if ok(t) and not last:
+            if t == 0:
+                softplus_end()
+            if ok(t):
                 st_zs(t)
             if ok(t + 1):
                 st_c(t + 1)
+            if t == -1:
+                softplus_ln()
             if ok(t + 2):
                 st_t(t + 2, 0)
-            if ok(t) and not last:
+            if ok(t):
                 st_vv(t)
             if ok(t + 2):
                 st_t(t + 2, 1)
-            if 0 <= t < NQ - 1:
-                st_idle()
+            if 1 <= t < NQ - 1 and 2 > 0:
+                st_dummy(2)
             if ok(t + 1):
                 st_qv(t + 1)
-                if ok(t - 1):
-                    st_e3(t - 1, sq[t + 1])
-                st_qs(t + 1)
-            if t == -1:
-                var_codes()
-            if t == 0:
-                load_k_table()
+                st_qs(t + 1, VSPLIT, J * D)
             if ok(t):
                 st_k(t)
             if ok(t + 1):

@@ -22,7 +22,7 @@ J = 4
 QROWS = P * J
 NQ = 16
 C = 128
-VSPLIT = 2112
+VSPLIT = 2304
 SIGN_BITS = -2147450880
 PRE = 5
 
@@ -74,9 +74,9 @@ def tile_bayesianoutputlayers_t_kernel(tc, x, cls_w, cls_b, sigma_w, bbox_w, bbo
         for q in range(PRE - 2):
             load(q)
         cb16 = prep.tile([P, C], BF16, name="cb16")
-        nc.scalar.dma_start(out=cb16[:], in_=cls_b.partition_broadcast(P))
+        nc.sync.dma_start(out=cb16[:], in_=cls_b.partition_broadcast(P))
         bb16 = prep.tile([P, C], BF16, name="bb16")
-        nc.scalar.dma_start(out=bb16[:], in_=bbox_b.partition_broadcast(P))
+        nc.sync.dma_start(out=bb16[:], in_=bbox_b.partition_broadcast(P))
 
         ident = const.tile([P, P], F32, name="ident")
         make_identity(nc, ident[:])

@@ -202,19 +202,6 @@ def tile_bayesianoutputlayers_t_kernel(tc, x, cls_w, cls_b, sigma_w, bbox_w, bbo
                     sl = slice((j * 2 + g) * P, (j * 2 + g + 1) * P)
                     mx(mb[q][:, j * C:(j + 1) * C], xc[q], xs[q], sl, wc, ws, slice(g * C, (g + 1) * C), g)
 
-        def st_dummy(n):
-            idle = ops.tile([P, 512], F32, name="wbank")
-            for i in range(n):
-                nc.tensor.matmul_mx(
-                    out=idle[:],
-                    lhsT=wc[:, 0:P].bitcast(FP8X4),
-                    lhsT_scale=ws[:, 0:P],
-                    rhs=wc[:].bitcast(FP8X4),
-                    rhs_scale=ws[:],
-                    start=True,
-                    stop=True,
-                )
-
         def st_vv(q):
             vb[q] = ops.tile([P, J * C], F32, name="vb")
             for j in range(J):
@@ -284,8 +271,6 @@ def tile_bayesianoutputlayers_t_kernel(tc, x, cls_w, cls_b, sigma_w, bbox_w, bbo
                 st_vv(t)
             if ok(t + 2):
                 st_t(t + 2, 1)
-            if 1 <= t < NQ - 1 and 2 > 0:
-                st_dummy(2)
             if ok(t + 1):
                 st_qv(t + 1)
                 st_qs(t + 1, VSPLIT, J * D)

import math
from contextlib import ExitStack

import concourse.mybir as mybir
from concourse.masks import make_identity

FLOPS = 3 * 2 * 8192 * 1024 * 128

F32 = mybir.dt.float32
BF16 = mybir.dt.bfloat16
U32 = mybir.dt.uint32
U8 = mybir.dt.uint8
I32 = mybir.dt.int32
FP8X4 = mybir.dt.float8_e4m3fn_x4
ACT = mybir.ActivationFunctionType
ALU = mybir.AluOpType

P = 128
D = 1024
WORDS = D // 2
J = 4
QROWS = P * J
NQ = 16
C = 128
VSPLIT = 2304
SIGN_BITS = -2147450880
PRE = 5


def tile_bayesianoutputlayers_t_kernel(tc, x, cls_w, cls_b, sigma_w, bbox_w, bbox_b, out_0, out_1):
    nc = tc.nc
    with ExitStack() as ctx:
        const = ctx.enter_context(tc.tile_pool(name="const", bufs=1))
        prep = ctx.enter_context(tc.tile_pool(name="prep", bufs=1))
        xin = ctx.enter_context(tc.tile_pool(name="xin", bufs=6))
        grp = ctx.enter_context(tc.tile_pool(name="grp", bufs=2))
        cod = ctx.enter_context(tc.tile_pool(name="cod", bufs=2))
        epi = ctx.enter_context(tc.tile_pool(name="epi", bufs=2))
        res = ctx.enter_context(tc.tile_pool(name="res", bufs=3))
        tps = ctx.enter_context(tc.psum_pool(name="tps", bufs=4))
        ops = ctx.enter_context(tc.psum_pool(name="ops", bufs=1))
        ctx.enter_context(tc.manual_schedule())

        xt = {}
        xg = {}
        sq = {}
        xc = {}
        xs = {}
        qc = {}
        qs = {}
        banks = {}
        mb = {}
        db = {}
        vb = {}
        kk = {}
        tm = {}

        def load(q):
            xt[q] = xin.tile([P, J * D], BF16, name="xt")
            rows = x[q * QROWS:(q + 1) * QROWS, :]
            if q == 0:
                view = rows.rearrange("(p j) k -> p j k", j=J)
                for j in range(J):
                    nc.sync.dma_start(out=xt[q][:, j * D:(j + 1) * D], in_=view[:, j, :])
            else:
                nc.sync.dma_start(out=xt[q][:], in_=rows.rearrange("(p j) k -> p (j k)", j=J))

        sg = prep.tile([P, D], BF16, name="sg")
        nc.sync.dma_start(out=sg[:], in_=sigma_w[:, :])
        cw = prep.tile([P, D], BF16, name="cw")
        nc.sync.dma_start(out=cw[:], in_=cls_w[:, :])
        bw = prep.tile([P, D], BF16, name="bw")
        nc.sync.dma_start(out=bw[:], in_=bbox_w[:, :])
        for q in range(PRE - 2):
            load(q)
        cb16 = prep.tile([P, C], BF16, name="cb16")
        nc.sync.dma_start(out=cb16[:], in_=cls_b.partition_broadcast(P))
        bb16 = prep.tile([P, C], BF16, name="bb16")
        nc.sync.dma_start(out=bb16[:], in_=bbox_b.partition_broadcast(P))

        ident = const.tile([P, P], F32, name="ident")
        make_identity(nc, ident[:])
        cbt = const.tile([P, C], F32, name="cbt")
        nc.gpsimd.tensor_copy(out=cbt[:], in_=cb16[:])
        bbt = const.tile([P, C], F32, name="bbt")
        nc.gpsimd.tensor_copy(out=bbt[:], in_=bb16[:])

        def transpose_row_tile(words, bank):
            for c in range(4):
                nc.tensor.transpose(bank[:, c * P:(c + 1) * P], words[:, c * P:(c + 1) * P], ident[:])

        def bank_view(bank):
            return bank[:].rearrange("p (g u r) -> p g r u", g=2, u=2, r=P)

        na = prep.tile([P, D], BF16, name="na")
        nc.vector.tensor_single_scalar(
            out=na[:].bitcast(I32), in_=sg[:].bitcast(I32), scalar=SIGN_BITS, op=ALU.bitwise_or
        )
        u = prep.tile([P, D], F32, name="u")
        nc.scalar.activation(out=u[:], in_=na[:], func=ACT.Exp)

        wg = const.tile([P, 2 * 2 * C * 4], BF16, name="wg", align_bytes=64)
        wgw = wg[:].bitcast(F32).rearrange("p (w g c u) -> p w g c u", w=2, g=2, c=C, u=2)
        for w, src, tag in ((0, cw, "mb"), (1, bw, "db")):
            wbank = ops.tile([P, WORDS], F32, name=tag)
            transpose_row_tile(src[:].bitcast(F32), wbank)
            nc.scalar.copy(out=wgw[:, w], in_=bank_view(wbank))
        q4 = prep.tile([P, D], F32, name="q4")
        nc.scalar.activation(out=q4[:], in_=na[:], func=ACT.Exp, scale=4.0, bias=1.0e-6 - math.log(4.0))

        a1 = prep.tile([P, D], F32, name="a1")
        nc.vector.tensor_scalar(out=a1[:], in0=u[:], scalar1=1.0 / 3.0, scalar2=-0.5, op0=ALU.mult, op1=ALU.add)
        a2 = prep.tile([P, D], F32, name="a2")
        nc.vector.tensor_tensor(out=a2[:], in0=a1[:], in1=u[:], op=ALU.mult)
        t3 = prep.tile([P, D], F32, name="t3")
        nc.vector.scalar_tensor_tensor(out=t3[:], in0=a2[:], scalar=1.0, in1=u[:], op0=ALU.add, op1=ALU.mult)
        wc = const.tile([P, 2 * 2 * C], U32, name="wc", align_bytes=64)
        ws = const.tile([P, 2 * 2 * C], U8, name="ws", align_bytes=64)
        nc.vector.quantize_mx(out=wc[:].bitcast(FP8X4), scales=ws[:], in_=wg[:])
        t4 = prep.tile([P, D], F32, name="t4")
        nc.vector.tensor_tensor(out=t4[:], in0=t3[:], in1=q4[:], op=ALU.subtract)
        lb = prep.tile([P, D], F32, name="lb")
        vc = const.tile([P, 2 * C], U32, name="vc", align_bytes=64)
        vs = const.tile([P, 2 * C], U8, name="vs", align_bytes=64)

        def softplus_ln():
            nc.scalar.activation(out=lb[:], in_=u[:], func=ACT.Ln, scale=1.0, bias=1.0)
            warm = prep.tile([P, 1], F32, name="warm")
            nc.scalar.activation(out=warm[:], in_=u[:, 0:1], func=ACT.Abs_reciprocal_sqrt, scale=1.0, bias=1.0)

        def softplus_end():
            m1 = prep.tile([P, D], F32, name="m1")
            nc.vector.tensor_tensor(out=m1[:], in0=t3[:], in1=lb[:], op=ALU.min)
            m2 = prep.tile([P, D], F32, name="m2")
            nc.vector.tensor_tensor(out=m2[:], in0=m1[:], in1=t4[:], op=ALU.max)
            vr = prep.tile([P, D], BF16, name="vr")
            nc.vector.scalar_tensor_tensor(out=vr[:], in0=sg[:], scalar=0.0, in1=m2[:], op0=ALU.max, op1=ALU.add)
            vg = const.tile([P, 2 * C * 4], BF16, name="vg", align_bytes=64)
            wbank = ops.tile([P, WORDS], F32, name="wbank")
            transpose_row_tile(vr[:].bitcast(F32), wbank)
            nc.vector.tensor_copy(
                out=vg[:].bitcast(F32).rearrange("p (g c u) -> p g c u", g=2, c=C, u=2), in_=bank_view(wbank)
            )
            nc.vector.quantize_mx(out=vc[:].bitcast(FP8X4), scales=vs[:], in_=vg[:])

        def st_t(q, half):
            xw = xt[q][:].bitcast(F32)
            if half == 0:
                banks[q] = []
            for j in range(2 * half, 2 * half + 2):
                bank = tps.tile([P, WORDS], F32, name="bank")
                transpose_row_tile(xw[:, j * WORDS:(j + 1) * WORDS], bank)
                banks[q].append(bank)

        def st_c(q):
            xg[q] = grp.tile([P, J * D], BF16, name="xg", align_bytes=64)
            xgw = xg[q][:].bitcast(F32).rearrange("p (j g r u) -> p j g r u", j=J, g=2, r=P, u=2)
            for j in range(J):
                nc.scalar.copy(out=xgw[:, j], in_=bank_view(banks[q][j]))
            sq[q] = grp.tile([P, J * D], BF16, name="sq", align_bytes=64)

        def st_qv(q):
            nc.vector.tensor_tensor(
                out=sq[q][:, :VSPLIT], in0=xg[q][:, :VSPLIT], in1=xg[q][:, :VSPLIT], op=ALU.mult
            )

        def st_qs(q, lo, hi):
            nc.scalar.activation(out=sq[q][:, lo:hi], in_=xg[q][:, lo:hi], func=ACT.Square)

        def st_zx(q):
            xc[q] = cod.tile([P, J * 2 * P], U32, name="xc", align_bytes=64)
            xs[q] = cod.tile([P, J * 2 * P], U8, name="xs", align_bytes=64)
            nc.vector.quantize_mx(out=xc[q][:].bitcast(FP8X4), scales=xs[q][:], in_=xg[q][:])

        def st_zs(q):
            qc[q] = cod.tile([P, J * 2 * P], U32, name="qc", align_bytes=64)
            qs[q] = cod.tile([P, J * 2 * P], U8, name="qs", align_bytes=64)
            nc.vector.quantize_mx(out=qc[q][:].bitcast(FP8X4), scales=qs[q][:], in_=sq[q][:])

        def mx(out, codes, scales, sl, wcodes, wscales, wsl, g):
            nc.tensor.matmul_mx(
                out=out,
                lhsT=codes[:, sl].bitcast(FP8X4),
                lhsT_scale=scales[:, sl],
                rhs=wcodes[:, wsl].bitcast(FP8X4),
                rhs_scale=wscales[:, wsl],
                start=(g == 0),
                stop=(g == 1),
            )

        def st_d(q):
            db[q] = ops.tile([P, J * C], F32, name="db")
            for j in range(J):
                for g in range(2):
                    sl = slice((j * 2 + g) * P, (j * 2 + g + 1) * P)
                    mx(db[q][:, j * C:(j + 1) * C], xc[q], xs[q], sl, wc, ws, slice((2 + g) * C, (3 + g) * C), g)

        def st_m(q):
            mb[q] = ops.tile([P, J * C], F32, name="mb")
            for j in range(J):
                for g in range(2):
                    sl = slice((j * 2 + g) * P, (j * 2 + g + 1) * P)
                    mx(mb[q][:, j * C:(j + 1) * C], xc[q], xs[q], sl, wc, ws, slice(g * C, (g + 1) * C), g)

        def st_vv(q):
            vb[q] = ops.tile([P, J * C], F32, name="vb")
            for j in range(J):
                for g in range(2):
                    sl = slice((j * 2 + g) * P, (j * 2 + g + 1) * P)
                    mx(vb[q][:, j * C:(j + 1) * C], qc[q], qs[q], sl, vc, vs, slice(g * C, (g + 1) * C), g)

        def st_k(q):
            kk[q] = epi.tile([P, J * C], F32, name="kk")
            nc.scalar.activation(
                out=kk[q][:], in_=vb[q][:], func=ACT.Abs_reciprocal_sqrt, scale=math.pi / 3200.0, bias=1.0 / 400.0
            )

        def st_e1(q):
            dl = res.tile([P, J * C], F32, name="dl")
            nc.vector.tensor_tensor(
                out=dl[:].rearrange("p (t c) -> p t c", t=J),
                in0=db[q][:].rearrange("p (t c) -> p t c", t=J),
                in1=bbt[:].unsqueeze(1).to_broadcast([P, J, C]),
                op=ALU.add,
            )
            nc.sync.dma_start(
                out=out_1[q * QROWS:(q + 1) * QROWS, :].rearrange("(p j) c -> p (j c)", j=J), in_=dl[:]
            )

        def st_e2(q):
            tm[q] = epi.tile([P, J * C], F32, name="tm")
            nc.vector.tensor_tensor(out=tm[q][:], in0=mb[q][:], in1=kk[q][:], op=ALU.mult)

        def st_e3(q):
            so = res.tile([P, J * C], F32, name="so")
            eng = nc.vector if (False or (True and q == NQ - 1)) else nc.gpsimd
            eng.tensor_tensor(
                out=so[:].rearrange("p (t c) -> p t c", t=J),
                in0=tm[q][:].rearrange("p (t c) -> p t c", t=J),
                in1=cbt[:].unsqueeze(1).to_broadcast([P, J, C]),
                op=ALU.add,
            )
            nc.sync.dma_start(
                out=out_0[q * QROWS:(q + 1) * QROWS, :].rearrange("(p j) c -> p (j c)", j=J), in_=so[:]
            )

        def ok(q):
            return 0 <= q < NQ

        for t in range(-2, NQ + 1):
            if PRE - 2 <= t + PRE < NQ:
                load(t + PRE)
            if ok(t):
                st_d(t)
            if ok(t - 1):
                st_e2(t - 1)
                st_e3(t - 1)
            if ok(t):
                st_m(t)
            if t == 0:
                softplus_end()
            if ok(t):
                st_zs(t)
            if ok(t + 1):
                st_c(t + 1)
            if t == -1:
                softplus_ln()
            if ok(t + 2):
                st_t(t + 2, 0)
            if ok(t):
                st_vv(t)
            if ok(t + 2):
                st_t(t + 2, 1)
            if ok(t + 1):
                st_qv(t + 1)
                st_qs(t + 1, VSPLIT, J * D)
            if ok(t):
                st_k(t)
            if ok(t + 1):
                st_zx(t + 1)
            if ok(t):
                st_e1(t)
